import numpy as np
import ml_dtypes

BF16 = ml_dtypes.bfloat16


def bf(x):
    return np.asarray(x, np.float32).astype(BF16)


def f32(x):
    return np.asarray(x, np.float32)


def f64(x):
    return np.asarray(x).astype(np.float64)


def striped(idx):
    return np.tile(idx.reshape(-1, 16).T, (8, 1))


C, S, N, H, K, E, M = 128, 1024, 2048, 512, 4, 16, 128
SLOPE = 0.2


def leaky(v):
    return np.maximum(v, 0.0) + SLOPE * np.minimum(v, 0.0)


def setup_inputs():
    return {
        "x": f32(np.random.standard_normal((C, S))),
        "edge": f32(np.random.uniform(size=(1, N))),
        "w_edge": f32(np.random.standard_normal((C, 1))),
        "attn_l": f32(np.random.standard_normal((C, 1)) / np.sqrt(C)),
        "attn_r": f32(0.5 * np.random.standard_normal((C, 1)) / np.sqrt(C)),
        "dst": f32(2.0 * np.random.standard_normal((C, M))),
        "offs": striped(np.concatenate([np.random.permutation(S)[:H] for _ in range(K)])),
    }


def reference(x, edge, w_edge, attn_l, attn_r, dst, offs):
    idx = offs[:16].T.reshape(-1)
    wmu = f64(x)[:, idx] + f64(w_edge) * f64(edge)
    s = (f64(attn_l) * wmu).sum(axis=0)
    er = (f64(attn_r) * f64(dst)).sum(axis=0)
    p = np.exp(leaky(s.reshape(M, E) + er[:, None]))
    pkk = np.exp(leaky(er + er))
    den = p.sum(axis=1) + pkk
    b = (wmu.reshape(C, M, E) * p[None, :, :]).sum(axis=2)
    z = (b + f64(dst) * pkk[None, :]) / den[None, :]
    return 1.0 / (1.0 + np.exp(-z))

@@ -1,0 +1,108 @@
+import concourse.mybir as mybir
+
+F32 = mybir.dt.float32
+BF16 = mybir.dt.bfloat16
+U16 = mybir.dt.uint16
+ALU = mybir.AluOpType
+FUNC = mybir.ActivationFunctionType
+AXIS = mybir.AxisListType
+
+C = 128
+S = 1024
+N = 2048
+M = 128
+E = 16
+PIECE = 512
+N_PIECES = N // PIECE
+MACH = PIECE // E
+SLOPE = 0.2
+
+FLOPS = 2 * C * N + 2 * C * M + 2 * C * N
+
+
+def tile_gatedge_kernel(tc, x, edge, w_edge, attn_l, attn_r, dst, offs, out):
+    nc = tc.nc
+    with (
+        tc.tile_pool(name="held", bufs=1) as held,
+        tc.tile_pool(name="work", bufs=2) as work,
+        tc.psum_pool(name="psum", bufs=2) as psum,
+    ):
+        offsets = held.tile([C, N // 16], U16, name="offsets")
+        nc.sync.dma_start(offsets[:], offs)
+        table = held.tile([C, S], F32, name="table")
+        nc.sync.dma_start(table[:], x)
+        edge_all = held.tile([C, N], F32, name="edge_all")
+        for r in range(N_PIECES):
+            cols = slice(r * PIECE, (r + 1) * PIECE)
+            nc.scalar.dma_start(edge_all[:, cols], edge[0, cols].partition_broadcast(C))
+        w_edge_col = held.tile([C, 1], F32, name="w_edge_col")
+        nc.gpsimd.dma_start(w_edge_col[:], w_edge)
+        attn_l_col = held.tile([C, 1], F32, name="attn_l_col")
+        nc.gpsimd.dma_start(attn_l_col[:], attn_l)
+        attn_r_col = held.tile([C, 1], F32, name="attn_r_col")
+        nc.gpsimd.dma_start(attn_r_col[:], attn_r)
+        dst_f32 = held.tile([C, M], F32, name="dst_f32")
+        nc.gpsimd.dma_start(dst_f32[:], dst)
+
+        attn_l_wide = held.tile([C, C], BF16, name="attn_l_wide")
+        nc.vector.tensor_copy(attn_l_wide[:], attn_l_col[:, 0:1].to_broadcast([C, C]))
+        attn_r_wide = held.tile([C, C], BF16, name="attn_r_wide")
+        nc.vector.tensor_copy(attn_r_wide[:], attn_r_col[:, 0:1].to_broadcast([C, C]))
+        dst_bf = held.tile([C, M], BF16, name="dst_bf")
+        nc.vector.tensor_copy(dst_bf[:], dst_f32[:])
+        er_ps = psum.tile([C, M], F32, name="er_ps")
+        nc.tensor.matmul(er_ps[:], attn_r_wide[:], dst_bf[:], start=True, stop=True)
+        er = held.tile([C, M], F32, name="er")
+        nc.vector.tensor_copy(er[:], er_ps[:])
+        pkk_pos = held.tile([C, M], F32, name="pkk_pos")
+        nc.scalar.activation(pkk_pos[:], er[:], FUNC.Exp, scale=2.0)
+        pkk_neg = held.tile([C, M], F32, name="pkk_neg")
+        nc.scalar.activation(pkk_neg[:], er[:], FUNC.Exp, scale=2.0 * SLOPE)
+        pkk = held.tile([C, M], F32, name="pkk")
+        nc.vector.tensor_tensor(pkk[:], pkk_pos[:], pkk_neg[:], ALU.max)
+
+        num = held.tile([C, M], F32, name="num")
+        den = held.tile([C, M], F32, name="den")
+        for r in range(N_PIECES):
+            cols = slice(r * PIECE, (r + 1) * PIECE)
+            machines = slice(r * MACH, (r + 1) * MACH)
+            we = work.tile([C, PIECE], F32, name="we")
+            nc.scalar.activation(we[:], edge_all[:, cols], FUNC.Copy, scale=w_edge_col[:, 0:1])
+            wmu = work.tile([C, PIECE], F32, name="wmu")
+            picked = table[:].indirect(offsets[:, r * (PIECE // 16) : (r + 1) * (PIECE // 16)])
+            nc.vector.tensor_tensor(wmu[:], picked, we[:], ALU.add)
+            wmu_bf = work.tile([C, PIECE], BF16, name="wmu_bf")
+            nc.scalar.copy(wmu_bf[:], wmu[:])
+            s_ps = psum.tile([C, PIECE], F32, name="s_ps")
+            nc.tensor.matmul(s_ps[:], attn_l_wide[:], wmu_bf[:], start=True, stop=True)
+            v = work.tile([C, MACH, E], F32, name="v")
+            nc.vector.tensor_tensor(
+                v[:],
+                s_ps[:].rearrange("c (m t) -> c m t", t=E),
+                er[:, machines].unsqueeze(2).to_broadcast([C, MACH, E]),
+                ALU.add,
+            )
+            p_pos = work.tile([C, MACH, E], F32, name="p_pos")
+            nc.scalar.activation(p_pos[:], v[:], FUNC.Exp)
+            p_neg = work.tile([C, MACH, E], F32, name="p_neg")
+            nc.scalar.activation(p_neg[:], v[:], FUNC.Exp, scale=SLOPE)
+            p = work.tile([C, MACH, E], F32, name="p")
+            nc.vector.tensor_tensor(p[:], p_pos[:], p_neg[:], ALU.max)
+            pw = work.tile([C, MACH, E], F32, name="pw")
+            nc.vector.tensor_tensor(pw[:], p[:], wmu[:].rearrange("c (m t) -> c m t", t=E), ALU.mult)
+            nc.vector.tensor_reduce(num[:, machines], pw[:], AXIS.X, ALU.add)
+            nc.vector.tensor_reduce(den[:, machines], p[:], AXIS.X, ALU.add)
+
+        own = held.tile([C, M], F32, name="own")
+        nc.vector.tensor_tensor(own[:], dst_f32[:], pkk[:], ALU.mult)
+        nc.vector.tensor_tensor(num[:], num[:], own[:], ALU.add)
+        nc.vector.tensor_tensor(den[:], den[:], pkk[:], ALU.add)
+        rden = held.tile([C, M], F32, name="rden")
+        nc.vector.reciprocal(rden[:], den[:])
+        z = held.tile([C, M], F32, name="z")
+        nc.vector.tensor_tensor(z[:], num[:], rden[:], ALU.mult)
+        half_tanh = held.tile([C, M], F32, name="half_tanh")
+        nc.scalar.activation(half_tanh[:], z[:], FUNC.Tanh, scale=0.5)
+        result = held.tile([C, M], F32, name="result")
+        nc.vector.tensor_scalar(result[:], half_tanh[:], 0.5, 0.5, ALU.mult, ALU.add)
+        nc.sync.dma_start(out, result[:])

@@ -1,4 +1,5 @@
 import concourse.mybir as mybir
+from concourse.masks import make_block_diagonal, make_identity
 
 F32 = mybir.dt.float32
 BF16 = mybir.dt.bfloat16
@@ -15,6 +16,9 @@ E = 16
 PIECE = 512
 N_PIECES = N // PIECE
 MACH = PIECE // E
+ROWS = 128
+BLOCKS = PIECE // ROWS
+SHARE = ROWS // MACH
 SLOPE = 0.2
 
 FLOPS = 2 * C * N + 2 * C * M + 2 * C * N
@@ -24,85 +28,131 @@ def tile_gatedge_kernel(tc, x, edge, w_edge, attn_l, attn_r, dst, offs, out):
     nc = tc.nc
     with (
         tc.tile_pool(name="held", bufs=1) as held,
-        tc.tile_pool(name="work", bufs=2) as work,
-        tc.psum_pool(name="psum", bufs=2) as psum,
+        tc.tile_pool(name="pieces", bufs=N_PIECES) as pieces,
+        tc.psum_pool(name="flip_banks", bufs=3) as flip_banks,
+        tc.psum_pool(name="small_banks", bufs=2) as small_banks,
+        tc.psum_pool(name="z_bank", bufs=1) as z_bank,
     ):
         offsets = held.tile([C, N // 16], U16, name="offsets")
         nc.sync.dma_start(offsets[:], offs)
         table = held.tile([C, S], F32, name="table")
         nc.sync.dma_start(table[:], x)
+        w_edge_col = held.tile([C, 1], F32, name="w_edge_col")
+        nc.scalar.dma_start(w_edge_col[:], w_edge)
         edge_all = held.tile([C, N], F32, name="edge_all")
         for r in range(N_PIECES):
             cols = slice(r * PIECE, (r + 1) * PIECE)
-            nc.scalar.dma_start(edge_all[:, cols], edge[0, cols].partition_broadcast(C))
-        w_edge_col = held.tile([C, 1], F32, name="w_edge_col")
-        nc.gpsimd.dma_start(w_edge_col[:], w_edge)
-        attn_l_col = held.tile([C, 1], F32, name="attn_l_col")
-        nc.gpsimd.dma_start(attn_l_col[:], attn_l)
-        attn_r_col = held.tile([C, 1], F32, name="attn_r_col")
-        nc.gpsimd.dma_start(attn_r_col[:], attn_r)
+            queue = nc.scalar if r == 0 else nc.sync
+            queue.dma_start(edge_all[:, cols], edge[0, cols].partition_broadcast(C))
         dst_f32 = held.tile([C, M], F32, name="dst_f32")
-        nc.gpsimd.dma_start(dst_f32[:], dst)
+        nc.scalar.dma_start(dst_f32[:], dst)
+        attn_r_col = held.tile([C, 1], F32, name="attn_r_col")
+        nc.scalar.dma_start(attn_r_col[:], attn_r)
+        attn_l_col = held.tile([C, 1], F32, name="attn_l_col")
+        nc.scalar.dma_start(attn_l_col[:], attn_l)
 
-        attn_l_wide = held.tile([C, C], BF16, name="attn_l_wide")
-        nc.vector.tensor_copy(attn_l_wide[:], attn_l_col[:, 0:1].to_broadcast([C, C]))
-        attn_r_wide = held.tile([C, C], BF16, name="attn_r_wide")
-        nc.vector.tensor_copy(attn_r_wide[:], attn_r_col[:, 0:1].to_broadcast([C, C]))
-        dst_bf = held.tile([C, M], BF16, name="dst_bf")
-        nc.vector.tensor_copy(dst_bf[:], dst_f32[:])
-        er_ps = psum.tile([C, M], F32, name="er_ps")
-        nc.tensor.matmul(er_ps[:], attn_r_wide[:], dst_bf[:], start=True, stop=True)
-        er = held.tile([C, M], F32, name="er")
-        nc.vector.tensor_copy(er[:], er_ps[:])
-        pkk_pos = held.tile([C, M], F32, name="pkk_pos")
-        nc.scalar.activation(pkk_pos[:], er[:], FUNC.Exp, scale=2.0)
-        pkk_neg = held.tile([C, M], F32, name="pkk_neg")
-        nc.scalar.activation(pkk_neg[:], er[:], FUNC.Exp, scale=2.0 * SLOPE)
-        pkk = held.tile([C, M], F32, name="pkk")
-        nc.vector.tensor_tensor(pkk[:], pkk_pos[:], pkk_neg[:], ALU.max)
-
-        num = held.tile([C, M], F32, name="num")
-        den = held.tile([C, M], F32, name="den")
+        we_of = []
         for r in range(N_PIECES):
-            cols = slice(r * PIECE, (r + 1) * PIECE)
-            machines = slice(r * MACH, (r + 1) * MACH)
-            we = work.tile([C, PIECE], F32, name="we")
-            nc.scalar.activation(we[:], edge_all[:, cols], FUNC.Copy, scale=w_edge_col[:, 0:1])
-            wmu = work.tile([C, PIECE], F32, name="wmu")
-            picked = table[:].indirect(offsets[:, r * (PIECE // 16) : (r + 1) * (PIECE // 16)])
-            nc.vector.tensor_tensor(wmu[:], picked, we[:], ALU.add)
-            wmu_bf = work.tile([C, PIECE], BF16, name="wmu_bf")
-            nc.scalar.copy(wmu_bf[:], wmu[:])
-            s_ps = psum.tile([C, PIECE], F32, name="s_ps")
-            nc.tensor.matmul(s_ps[:], attn_l_wide[:], wmu_bf[:], start=True, stop=True)
-            v = work.tile([C, MACH, E], F32, name="v")
-            nc.vector.tensor_tensor(
-                v[:],
-                s_ps[:].rearrange("c (m t) -> c m t", t=E),
-                er[:, machines].unsqueeze(2).to_broadcast([C, MACH, E]),
-                ALU.add,
+            we = pieces.tile([C, PIECE], F32, name="we")
+            nc.scalar.activation(
+                we[:], edge_all[:, r * PIECE : (r + 1) * PIECE], FUNC.Copy, scale=w_edge_col[:, 0:1]
             )
-            p_pos = work.tile([C, MACH, E], F32, name="p_pos")
-            nc.scalar.activation(p_pos[:], v[:], FUNC.Exp)
-            p_neg = work.tile([C, MACH, E], F32, name="p_neg")
-            nc.scalar.activation(p_neg[:], v[:], FUNC.Exp, scale=SLOPE)
-            p = work.tile([C, MACH, E], F32, name="p")
-            nc.vector.tensor_tensor(p[:], p_pos[:], p_neg[:], ALU.max)
-            pw = work.tile([C, MACH, E], F32, name="pw")
-            nc.vector.tensor_tensor(pw[:], p[:], wmu[:].rearrange("c (m t) -> c m t", t=E), ALU.mult)
-            nc.vector.tensor_reduce(num[:, machines], pw[:], AXIS.X, ALU.add)
-            nc.vector.tensor_reduce(den[:, machines], p[:], AXIS.X, ALU.add)
+            we_of.append(we)
 
-        own = held.tile([C, M], F32, name="own")
-        nc.vector.tensor_tensor(own[:], dst_f32[:], pkk[:], ALU.mult)
-        nc.vector.tensor_tensor(num[:], num[:], own[:], ALU.add)
-        nc.vector.tensor_tensor(den[:], den[:], pkk[:], ALU.add)
-        rden = held.tile([C, M], F32, name="rden")
-        nc.vector.reciprocal(rden[:], den[:])
-        z = held.tile([C, M], F32, name="z")
-        nc.vector.tensor_tensor(z[:], num[:], rden[:], ALU.mult)
+        identity = held.tile([C, C], F32, name="identity")
+        make_identity(nc, identity[:])
+        same_machine = held.tile([ROWS, ROWS], F32, name="same_machine")
+        make_block_diagonal(nc, same_machine[:], SHARE)
+        row_of_machine = same_machine[:].rearrange("i (m u) -> i u m", u=SHARE)[:, 0, :]
+
+        attn_l_bf = held.tile([C, 1], BF16, name="attn_l_bf")
+        nc.vector.tensor_copy(attn_l_bf[:], attn_l_col[:])
+        attn_r_bf = held.tile([C, 1], BF16, name="attn_r_bf")
+        nc.vector.tensor_copy(attn_r_bf[:], attn_r_col[:])
+
+        dst_wide = dst_f32[:].unsqueeze(2).to_broadcast([C, M, SHARE])
+        dst_rep = held.tile([C, M, SHARE], F32, name="dst_rep")
+        nc.vector.tensor_copy(dst_rep[:], dst_wide)
+        dst_rep_bf = held.tile([C, M, SHARE], BF16, name="dst_rep_bf")
+        nc.vector.tensor_copy(dst_rep_bf[:], dst_wide)
+        dst_rep_blocks = dst_rep[:].rearrange("c m u -> c (m u)")
+        dst_rep_bf_blocks = dst_rep_bf[:].rearrange("c m u -> c (m u)")
+        er_ps = small_banks.tile([ROWS, N_PIECES], F32, name="er_ps", tag="scores")
+        dst_flipped = flip_banks.tile([ROWS, N_PIECES, C], F32, name="dst_flipped", tag="flipped")
+        for r in range(N_PIECES):
+            rows = slice(r * ROWS, (r + 1) * ROWS)
+            nc.tensor.matmul(er_ps[:, r : r + 1], dst_rep_bf_blocks[:, rows], attn_r_bf[:], start=True, stop=True)
+            nc.tensor.transpose(dst_flipped[:, r, :], dst_rep_blocks[:, rows], identity[:])
+        er = held.tile([ROWS, N_PIECES], F32, name="er")
+        nc.scalar.copy(er[:], er_ps[:])
+        er_slope = held.tile([ROWS, N_PIECES], F32, name="er_slope")
+        nc.scalar.mul(er_slope[:], er_ps[:], SLOPE)
+        pkk_pos = held.tile([ROWS, N_PIECES], F32, name="pkk_pos")
+        nc.scalar.activation(pkk_pos[:], er_ps[:], FUNC.Exp, scale=2.0)
+        pkk_neg = held.tile([ROWS, N_PIECES], F32, name="pkk_neg")
+        nc.scalar.activation(pkk_neg[:], er_ps[:], FUNC.Exp, scale=2.0 * SLOPE)
+        pkk = held.tile([ROWS, N_PIECES], F32, name="pkk")
+        nc.vector.tensor_tensor(pkk[:], pkk_pos[:], pkk_neg[:], ALU.max)
+        weights = held.tile([ROWS, N_PIECES, BLOCKS + 1], F32, name="weights")
+        nc.vector.tensor_scalar(weights[:, :, BLOCKS], pkk[:], 1.0 / SHARE, None, ALU.mult)
+        acc_of = []
+        for r in range(N_PIECES):
+            acc = pieces.tile([ROWS, C], F32, name="acc")
+            nc.scalar.activation(acc[:], dst_flipped[:, r, :], FUNC.Copy, scale=weights[:, r, BLOCKS : BLOCKS + 1])
+            acc_of.append(acc)
+
+        z_ps = z_bank.tile([C, M], F32, name="z_ps")
+        flipped_of = []
+        p_pos_of = []
+        p_neg_of = []
+
+        def look_up(r):
+            wmu = pieces.tile([C, PIECE], F32, name="wmu")
+            picked = table[:].indirect(offsets[:, r * (PIECE // 16) : (r + 1) * (PIECE // 16)])
+            nc.vector.tensor_tensor(wmu[:], picked, we_of[r][:], ALU.add)
+            wmu_bf = pieces.tile([C, PIECE], BF16, name="wmu_bf")
+            nc.scalar.copy(wmu_bf[:], wmu[:])
+            wmu_blocks = wmu[:].rearrange("c (i a) -> c a i", a=BLOCKS)
+            wmu_bf_blocks = wmu_bf[:].rearrange("c (i a) -> c a i", a=BLOCKS)
+            flipped = flip_banks.tile([ROWS, BLOCKS, C], F32, name="flipped", tag="flipped")
+            scores = small_banks.tile([ROWS, BLOCKS], F32, name="scores", tag="scores")
+            for a in range(BLOCKS):
+                nc.tensor.transpose(flipped[:, a, :], wmu_blocks[:, a, :], identity[:])
+            for a in range(BLOCKS):
+                nc.tensor.matmul(scores[:, a : a + 1], wmu_bf_blocks[:, a, :], attn_l_bf[:], start=True, stop=True)
+            p_pos = pieces.tile([ROWS, BLOCKS], F32, name="p_pos")
+            nc.scalar.activation(p_pos[:], scores[:], FUNC.Exp, bias=er[:, r : r + 1], scale=1.0)
+            p_neg = pieces.tile([ROWS, BLOCKS], F32, name="p_neg")
+            nc.scalar.activation(p_neg[:], scores[:], FUNC.Exp, bias=er_slope[:, r : r + 1], scale=SLOPE)
+            flipped_of.append(flipped)
+            p_pos_of.append(p_pos)
+            p_neg_of.append(p_neg)
+
+        def weigh(r):
+            flipped, acc = flipped_of[r], acc_of[r]
+            nc.vector.tensor_tensor(weights[:, r, 0:BLOCKS], p_pos_of[r][:], p_neg_of[r][:], ALU.max)
+            row_sum = pieces.tile([ROWS, 1], F32, name="row_sum")
+            nc.vector.tensor_reduce(row_sum[:], weights[:, r, :], AXIS.X, ALU.add)
+            den_ps = small_banks.tile([ROWS, 1], F32, name="den_ps", tag="den")
+            nc.tensor.matmul(den_ps[:], same_machine[:], row_sum[:], start=True, stop=True)
+            for a in range(BLOCKS):
+                nc.vector.scalar_tensor_tensor(
+                    acc[:], flipped[:, a, :], weights[:, r, a : a + 1], acc[:], ALU.mult, ALU.add
+                )
+            rden = pieces.tile([ROWS, 1], F32, name="rden")
+            nc.vector.reciprocal(rden[:], den_ps[:])
+            fold = pieces.tile([ROWS, MACH], F32, name="fold")
+            nc.vector.tensor_scalar(fold[:], row_of_machine, rden[:, 0:1], None, ALU.mult)
+            nc.tensor.matmul(z_ps[:, r * MACH : (r + 1) * MACH], acc[:], fold[:], start=True, stop=True)
+
+        look_up(0)
+        for r in range(1, N_PIECES):
+            look_up(r)
+            weigh(r - 1)
+        weigh(N_PIECES - 1)
+
         half_tanh = held.tile([C, M], F32, name="half_tanh")
-        nc.scalar.activation(half_tanh[:], z[:], FUNC.Tanh, scale=0.5)
+        nc.scalar.activation(half_tanh[:], z_ps[:], FUNC.Tanh, scale=0.5)
         result = held.tile([C, M], F32, name="result")
         nc.vector.tensor_scalar(result[:], half_tanh[:], 0.5, 0.5, ALU.mult, ALU.add)
         nc.sync.dma_start(out, result[:])

@@ -29,35 +29,29 @@ def tile_gatedge_kernel(tc, x, edge, w_edge, attn_l, attn_r, dst, offs, out):
     with (
         tc.tile_pool(name="held", bufs=1) as held,
         tc.tile_pool(name="pieces", bufs=N_PIECES) as pieces,
-        tc.psum_pool(name="flip_banks", bufs=3) as flip_banks,
-        tc.psum_pool(name="small_banks", bufs=2) as small_banks,
-        tc.psum_pool(name="z_bank", bufs=1) as z_bank,
+        tc.psum_pool(name="flip_banks", bufs=N_PIECES) as flip_banks,
+        tc.psum_pool(name="score_banks", bufs=2) as score_banks,
+        tc.psum_pool(name="single_banks", bufs=1) as single_banks,
     ):
-        offsets = held.tile([C, N // 16], U16, name="offsets")
-        nc.sync.dma_start(offsets[:], offs)
+        scratch = held.tile([C, 1], F32, name="scratch")
+        nc.gpsimd.memset(scratch[:], 0.0)
+        nc.scalar.activation(scratch[:], scratch[:], FUNC.Exp)
+
         table = held.tile([C, S], F32, name="table")
         nc.sync.dma_start(table[:], x)
+        offsets = held.tile([C, N // 16], U16, name="offsets")
+        nc.sync.dma_start(offsets[:], offs)
+        edge_all = held.tile([C, N], F32, name="edge_all")
+        nc.scalar.dma_start(edge_all[:, 0:PIECE], edge[0, 0:PIECE].partition_broadcast(C))
         w_edge_col = held.tile([C, 1], F32, name="w_edge_col")
         nc.scalar.dma_start(w_edge_col[:], w_edge)
-        edge_all = held.tile([C, N], F32, name="edge_all")
-        for r in range(N_PIECES):
-            cols = slice(r * PIECE, (r + 1) * PIECE)
-            queue = nc.scalar if r == 0 else nc.sync
-            queue.dma_start(edge_all[:, cols], edge[0, cols].partition_broadcast(C))
         dst_f32 = held.tile([C, M], F32, name="dst_f32")
-        nc.scalar.dma_start(dst_f32[:], dst)
+        nc.sync.dma_start(dst_f32[:], dst)
         attn_r_col = held.tile([C, 1], F32, name="attn_r_col")
-        nc.scalar.dma_start(attn_r_col[:], attn_r)
+        nc.sync.dma_start(attn_r_col[:], attn_r)
+        nc.scalar.dma_start(edge_all[:, PIECE:N], edge[0, PIECE:N].partition_broadcast(C))
         attn_l_col = held.tile([C, 1], F32, name="attn_l_col")
-        nc.scalar.dma_start(attn_l_col[:], attn_l)
-
-        we_of = []
-        for r in range(N_PIECES):
-            we = pieces.tile([C, PIECE], F32, name="we")
-            nc.scalar.activation(
-                we[:], edge_all[:, r * PIECE : (r + 1) * PIECE], FUNC.Copy, scale=w_edge_col[:, 0:1]
-            )
-            we_of.append(we)
+        nc.sync.dma_start(attn_l_col[:], attn_l)
 
         identity = held.tile([C, C], F32, name="identity")
         make_identity(nc, identity[:])
@@ -65,46 +59,64 @@ def tile_gatedge_kernel(tc, x, edge, w_edge, attn_l, attn_r, dst, offs, out):
         make_block_diagonal(nc, same_machine[:], SHARE)
         row_of_machine = same_machine[:].rearrange("i (m u) -> i u m", u=SHARE)[:, 0, :]
 
-        attn_l_bf = held.tile([C, 1], BF16, name="attn_l_bf")
-        nc.vector.tensor_copy(attn_l_bf[:], attn_l_col[:])
-        attn_r_bf = held.tile([C, 1], BF16, name="attn_r_bf")
-        nc.vector.tensor_copy(attn_r_bf[:], attn_r_col[:])
-
-        dst_wide = dst_f32[:].unsqueeze(2).to_broadcast([C, M, SHARE])
-        dst_rep = held.tile([C, M, SHARE], F32, name="dst_rep")
-        nc.vector.tensor_copy(dst_rep[:], dst_wide)
-        dst_rep_bf = held.tile([C, M, SHARE], BF16, name="dst_rep_bf")
-        nc.vector.tensor_copy(dst_rep_bf[:], dst_wide)
-        dst_rep_blocks = dst_rep[:].rearrange("c m u -> c (m u)")
-        dst_rep_bf_blocks = dst_rep_bf[:].rearrange("c m u -> c (m u)")
-        er_ps = small_banks.tile([ROWS, N_PIECES], F32, name="er_ps", tag="scores")
-        dst_flipped = flip_banks.tile([ROWS, N_PIECES, C], F32, name="dst_flipped", tag="flipped")
-        for r in range(N_PIECES):
-            rows = slice(r * ROWS, (r + 1) * ROWS)
-            nc.tensor.matmul(er_ps[:, r : r + 1], dst_rep_bf_blocks[:, rows], attn_r_bf[:], start=True, stop=True)
-            nc.tensor.transpose(dst_flipped[:, r, :], dst_rep_blocks[:, rows], identity[:])
         er = held.tile([ROWS, N_PIECES], F32, name="er")
-        nc.scalar.copy(er[:], er_ps[:])
         er_slope = held.tile([ROWS, N_PIECES], F32, name="er_slope")
-        nc.scalar.mul(er_slope[:], er_ps[:], SLOPE)
-        pkk_pos = held.tile([ROWS, N_PIECES], F32, name="pkk_pos")
-        nc.scalar.activation(pkk_pos[:], er_ps[:], FUNC.Exp, scale=2.0)
-        pkk_neg = held.tile([ROWS, N_PIECES], F32, name="pkk_neg")
-        nc.scalar.activation(pkk_neg[:], er_ps[:], FUNC.Exp, scale=2.0 * SLOPE)
-        pkk = held.tile([ROWS, N_PIECES], F32, name="pkk")
-        nc.vector.tensor_tensor(pkk[:], pkk_pos[:], pkk_neg[:], ALU.max)
+        p_pos = held.tile([ROWS, N_PIECES, BLOCKS], F32, name="p_pos")
+        p_neg = held.tile([ROWS, N_PIECES, BLOCKS], F32, name="p_neg")
         weights = held.tile([ROWS, N_PIECES, BLOCKS + 1], F32, name="weights")
-        nc.vector.tensor_scalar(weights[:, :, BLOCKS], pkk[:], 1.0 / SHARE, None, ALU.mult)
+        row_sum = held.tile([ROWS, N_PIECES], F32, name="row_sum")
+        rden = held.tile([ROWS, N_PIECES], F32, name="rden")
+        fold = held.tile([ROWS, N_PIECES, MACH], F32, name="fold")
+        den_ps = single_banks.tile([ROWS, N_PIECES], F32, name="den_ps")
+        z_ps = single_banks.tile([C, M], F32, name="z_ps")
+        dst_flipped = flip_banks.tile([ROWS, N_PIECES, C], F32, name="dst_flipped", tag="flipped")
+        pkk_pos = held.tile([ROWS, N_PIECES], F32, name="pkk_pos")
+        pkk_neg = held.tile([ROWS, N_PIECES], F32, name="pkk_neg")
+        attn_l_bf = held.tile([C, 1], BF16, name="attn_l_bf")
+        we_of = []
         acc_of = []
-        for r in range(N_PIECES):
+        flipped_of = []
+        scores_of = []
+
+        def scale_edge(r):
+            we = pieces.tile([C, PIECE], F32, name="we")
+            nc.scalar.activation(
+                we[:], edge_all[:, r * PIECE : (r + 1) * PIECE], FUNC.Copy, scale=w_edge_col[:, 0:1]
+            )
+            we_of.append(we)
+
+        def own_scores():
+            attn_r_bf = held.tile([C, 1], BF16, name="attn_r_bf")
+            nc.gpsimd.tensor_copy(attn_r_bf[:], attn_r_col[:])
+            dst_wide = dst_f32[:].unsqueeze(2).to_broadcast([C, M, SHARE])
+            dst_rep_bf = held.tile([C, M, SHARE], BF16, name="dst_rep_bf")
+            nc.vector.tensor_copy(dst_rep_bf[:], dst_wide)
+            dst_rep = held.tile([C, M, SHARE], F32, name="dst_rep")
+            nc.vector.tensor_copy(dst_rep[:], dst_wide)
+            nc.gpsimd.tensor_copy(attn_l_bf[:], attn_l_col[:])
+            dst_rep_bf_blocks = dst_rep_bf[:].rearrange("c m u -> c (m u)")
+            dst_rep_blocks = dst_rep[:].rearrange("c m u -> c (m u)")
+            er_ps = score_banks.tile([ROWS, N_PIECES], F32, name="er_ps", tag="scores")
+            for r in range(N_PIECES):
+                rows = slice(r * ROWS, (r + 1) * ROWS)
+                nc.tensor.matmul(er_ps[:, r : r + 1], dst_rep_bf_blocks[:, rows], attn_r_bf[:], start=True, stop=True)
+            for r in range(N_PIECES):
+                rows = slice(r * ROWS, (r + 1) * ROWS)
+                nc.tensor.transpose(dst_flipped[:, r, :], dst_rep_blocks[:, rows], identity[:])
+            nc.scalar.copy(er[:], er_ps[:])
+            nc.scalar.mul(er_slope[:], er_ps[:], SLOPE)
+            nc.scalar.activation(pkk_pos[:], er_ps[:], FUNC.Exp, scale=2.0)
+            nc.scalar.activation(pkk_neg[:], er_ps[:], FUNC.Exp, scale=2.0 * SLOPE)
+
+        def own_weights():
+            pkk = held.tile([ROWS, N_PIECES], F32, name="pkk")
+            nc.vector.tensor_tensor(pkk[:], pkk_pos[:], pkk_neg[:], ALU.max)
+            nc.vector.tensor_scalar(weights[:, :, BLOCKS], pkk[:], 1.0 / SHARE, None, ALU.mult)
+
+        def own_rows(r):
             acc = pieces.tile([ROWS, C], F32, name="acc")
             nc.scalar.activation(acc[:], dst_flipped[:, r, :], FUNC.Copy, scale=weights[:, r, BLOCKS : BLOCKS + 1])
             acc_of.append(acc)
-
-        z_ps = z_bank.tile([C, M], F32, name="z_ps")
-        flipped_of = []
-        p_pos_of = []
-        p_neg_of = []
 
         def look_up(r):
             wmu = pieces.tile([C, PIECE], F32, name="wmu")
@@ -115,44 +127,59 @@ def tile_gatedge_kernel(tc, x, edge, w_edge, attn_l, attn_r, dst, offs, out):
             wmu_blocks = wmu[:].rearrange("c (i a) -> c a i", a=BLOCKS)
             wmu_bf_blocks = wmu_bf[:].rearrange("c (i a) -> c a i", a=BLOCKS)
             flipped = flip_banks.tile([ROWS, BLOCKS, C], F32, name="flipped", tag="flipped")
-            scores = small_banks.tile([ROWS, BLOCKS], F32, name="scores", tag="scores")
+            scores = score_banks.tile([ROWS, BLOCKS], F32, name="scores", tag="scores")
             for a in range(BLOCKS):
                 nc.tensor.transpose(flipped[:, a, :], wmu_blocks[:, a, :], identity[:])
             for a in range(BLOCKS):
                 nc.tensor.matmul(scores[:, a : a + 1], wmu_bf_blocks[:, a, :], attn_l_bf[:], start=True, stop=True)
-            p_pos = pieces.tile([ROWS, BLOCKS], F32, name="p_pos")
-            nc.scalar.activation(p_pos[:], scores[:], FUNC.Exp, bias=er[:, r : r + 1], scale=1.0)
-            p_neg = pieces.tile([ROWS, BLOCKS], F32, name="p_neg")
-            nc.scalar.activation(p_neg[:], scores[:], FUNC.Exp, bias=er_slope[:, r : r + 1], scale=SLOPE)
             flipped_of.append(flipped)
-            p_pos_of.append(p_pos)
-            p_neg_of.append(p_neg)
+            scores_of.append(scores)
 
-        def weigh(r):
-            flipped, acc = flipped_of[r], acc_of[r]
-            nc.vector.tensor_tensor(weights[:, r, 0:BLOCKS], p_pos_of[r][:], p_neg_of[r][:], ALU.max)
-            row_sum = pieces.tile([ROWS, 1], F32, name="row_sum")
-            nc.vector.tensor_reduce(row_sum[:], weights[:, r, :], AXIS.X, ALU.add)
-            den_ps = small_banks.tile([ROWS, 1], F32, name="den_ps", tag="den")
-            nc.tensor.matmul(den_ps[:], same_machine[:], row_sum[:], start=True, stop=True)
+        def exponentials(r):
+            nc.scalar.activation(p_pos[:, r, :], scores_of[r][:], FUNC.Exp, bias=er[:, r : r + 1], scale=1.0)
+            nc.scalar.activation(p_neg[:, r, :], scores_of[r][:], FUNC.Exp, bias=er_slope[:, r : r + 1], scale=SLOPE)
+
+        def weigh(first, count):
+            group = slice(first, first + count)
+            nc.vector.tensor_tensor(weights[:, group, 0:BLOCKS], p_pos[:, group, :], p_neg[:, group, :], ALU.max)
+            nc.vector.tensor_reduce(row_sum[:, group], weights[:, group, :], AXIS.X, ALU.add)
+            nc.tensor.matmul(den_ps[:, group], same_machine[:], row_sum[:, group], start=True, stop=True)
             for a in range(BLOCKS):
-                nc.vector.scalar_tensor_tensor(
-                    acc[:], flipped[:, a, :], weights[:, r, a : a + 1], acc[:], ALU.mult, ALU.add
-                )
-            rden = pieces.tile([ROWS, 1], F32, name="rden")
-            nc.vector.reciprocal(rden[:], den_ps[:])
-            fold = pieces.tile([ROWS, MACH], F32, name="fold")
-            nc.vector.tensor_scalar(fold[:], row_of_machine, rden[:, 0:1], None, ALU.mult)
-            nc.tensor.matmul(z_ps[:, r * MACH : (r + 1) * MACH], acc[:], fold[:], start=True, stop=True)
+                for r in range(first, first + count):
+                    nc.vector.scalar_tensor_tensor(
+                        acc_of[r][:], flipped_of[r][:, a, :], weights[:, r, a : a + 1], acc_of[r][:], ALU.mult, ALU.add
+                    )
+            nc.vector.reciprocal(rden[:, group], den_ps[:, group])
+            nc.vector.tensor_tensor(
+                fold[:, group, :],
+                row_of_machine.unsqueeze(1).to_broadcast([ROWS, count, MACH]),
+                rden[:, group].unsqueeze(2).to_broadcast([ROWS, count, MACH]),
+                ALU.mult,
+            )
+            for r in range(first, first + count):
+                nc.tensor.matmul(z_ps[:, r * MACH : (r + 1) * MACH], acc_of[r][:], fold[:, r, :], start=True, stop=True)
 
+        scale_edge(0)
+        scale_edge(1)
+        own_scores()
+        scale_edge(2)
         look_up(0)
-        for r in range(1, N_PIECES):
-            look_up(r)
-            weigh(r - 1)
-        weigh(N_PIECES - 1)
+        own_weights()
+        scale_edge(3)
+        own_rows(0)
+        own_rows(1)
+        look_up(1)
+        exponentials(0)
+        own_rows(2)
+        own_rows(3)
+        look_up(2)
+        exponentials(1)
+        look_up(3)
+        exponentials(2)
+        exponentials(3)
+        weigh(0, 2)
+        weigh(2, 2)
 
-        half_tanh = held.tile([C, M], F32, name="half_tanh")
-        nc.scalar.activation(half_tanh[:], z_ps[:], FUNC.Tanh, scale=0.5)
         result = held.tile([C, M], F32, name="result")
-        nc.vector.tensor_scalar(result[:], half_tanh[:], 0.5, 0.5, ALU.mult, ALU.add)
+        nc.scalar.activation(result[:], z_ps[:], FUNC.Sigmoid)
         nc.sync.dma_start(out, result[:])

@@ -33,31 +33,41 @@ def tile_gatedge_kernel(tc, x, edge, w_edge, attn_l, attn_r, dst, offs, out):
         tc.psum_pool(name="score_banks", bufs=2) as score_banks,
         tc.psum_pool(name="single_banks", bufs=1) as single_banks,
     ):
-        scratch = held.tile([C, 1], F32, name="scratch")
-        nc.gpsimd.memset(scratch[:], 0.0)
-        nc.scalar.activation(scratch[:], scratch[:], FUNC.Exp)
-
+        vector_rows = held.tile([1, 3 * C], F32, name="vector_rows")
+        nc.scalar.dma_start(vector_rows[:, 0:C], w_edge.rearrange("c one -> one c"))
         table = held.tile([C, S], F32, name="table")
         nc.sync.dma_start(table[:], x)
         offsets = held.tile([C, N // 16], U16, name="offsets")
         nc.sync.dma_start(offsets[:], offs)
         edge_all = held.tile([C, N], F32, name="edge_all")
         nc.scalar.dma_start(edge_all[:, 0:PIECE], edge[0, 0:PIECE].partition_broadcast(C))
-        w_edge_col = held.tile([C, 1], F32, name="w_edge_col")
-        nc.scalar.dma_start(w_edge_col[:], w_edge)
+        scratch = held.tile([C, 1], F32, name="scratch")
+        nc.gpsimd.memset(scratch[:], 0.0)
+        nc.scalar.activation(scratch[:], scratch[:], FUNC.Exp)
         dst_f32 = held.tile([C, M], F32, name="dst_f32")
-        nc.sync.dma_start(dst_f32[:], dst)
-        attn_r_col = held.tile([C, 1], F32, name="attn_r_col")
-        nc.sync.dma_start(attn_r_col[:], attn_r)
+        nc.scalar.dma_start(dst_f32[:], dst)
+        nc.sync.dma_start(vector_rows[:, C : 2 * C], attn_r.rearrange("c one -> one c"))
+        nc.sync.dma_start(vector_rows[:, 2 * C : 3 * C], attn_l.rearrange("c one -> one c"))
         nc.scalar.dma_start(edge_all[:, PIECE:N], edge[0, PIECE:N].partition_broadcast(C))
-        attn_l_col = held.tile([C, 1], F32, name="attn_l_col")
-        nc.sync.dma_start(attn_l_col[:], attn_l)
 
         identity = held.tile([C, C], F32, name="identity")
         make_identity(nc, identity[:])
         same_machine = held.tile([ROWS, ROWS], F32, name="same_machine")
         make_block_diagonal(nc, same_machine[:], SHARE)
         row_of_machine = same_machine[:].rearrange("i (m u) -> i u m", u=SHARE)[:, 0, :]
+
+        one = held.tile([1, 1], F32, name="one")
+        nc.vector.memset(one[:], 1.0)
+        w_edge_ps = score_banks.tile([C, 1], F32, name="w_edge_ps", tag="scores")
+        nc.tensor.matmul(w_edge_ps[:], vector_rows[:, 0:C], one[:], start=True, stop=True)
+        w_edge_col = held.tile([C, 1], F32, name="w_edge_col")
+        nc.vector.tensor_copy(w_edge_col[:], w_edge_ps[:])
+        attn_ps = score_banks.tile([C, 2], F32, name="attn_ps", tag="scores")
+        for k in range(2):
+            nc.tensor.matmul(attn_ps[:, k : k + 1], vector_rows[:, (k + 1) * C : (k + 2) * C], one[:], start=True, stop=True)
+        attn_bf = held.tile([C, 2], BF16, name="attn_bf")
+        attn_r_bf = attn_bf[:, 0:1]
+        attn_l_bf = attn_bf[:, 1:2]
 
         er = held.tile([ROWS, N_PIECES], F32, name="er")
         er_slope = held.tile([ROWS, N_PIECES], F32, name="er_slope")
@@ -72,7 +82,6 @@ def tile_gatedge_kernel(tc, x, edge, w_edge, attn_l, attn_r, dst, offs, out):
         dst_flipped = flip_banks.tile([ROWS, N_PIECES, C], F32, name="dst_flipped", tag="flipped")
         pkk_pos = held.tile([ROWS, N_PIECES], F32, name="pkk_pos")
         pkk_neg = held.tile([ROWS, N_PIECES], F32, name="pkk_neg")
-        attn_l_bf = held.tile([C, 1], BF16, name="attn_l_bf")
         we_of = []
         acc_of = []
         flipped_of = []
@@ -86,20 +95,17 @@ def tile_gatedge_kernel(tc, x, edge, w_edge, attn_l, attn_r, dst, offs, out):
             we_of.append(we)
 
         def own_scores():
-            attn_r_bf = held.tile([C, 1], BF16, name="attn_r_bf")
-            nc.gpsimd.tensor_copy(attn_r_bf[:], attn_r_col[:])
             dst_wide = dst_f32[:].unsqueeze(2).to_broadcast([C, M, SHARE])
             dst_rep_bf = held.tile([C, M, SHARE], BF16, name="dst_rep_bf")
             nc.vector.tensor_copy(dst_rep_bf[:], dst_wide)
             dst_rep = held.tile([C, M, SHARE], F32, name="dst_rep")
             nc.vector.tensor_copy(dst_rep[:], dst_wide)
-            nc.gpsimd.tensor_copy(attn_l_bf[:], attn_l_col[:])
             dst_rep_bf_blocks = dst_rep_bf[:].rearrange("c m u -> c (m u)")
             dst_rep_blocks = dst_rep[:].rearrange("c m u -> c (m u)")
             er_ps = score_banks.tile([ROWS, N_PIECES], F32, name="er_ps", tag="scores")
             for r in range(N_PIECES):
                 rows = slice(r * ROWS, (r + 1) * ROWS)
-                nc.tensor.matmul(er_ps[:, r : r + 1], dst_rep_bf_blocks[:, rows], attn_r_bf[:], start=True, stop=True)
+                nc.tensor.matmul(er_ps[:, r : r + 1], dst_rep_bf_blocks[:, rows], attn_r_bf, start=True, stop=True)
             for r in range(N_PIECES):
                 rows = slice(r * ROWS, (r + 1) * ROWS)
                 nc.tensor.transpose(dst_flipped[:, r, :], dst_rep_blocks[:, rows], identity[:])
@@ -131,7 +137,7 @@ def tile_gatedge_kernel(tc, x, edge, w_edge, attn_l, attn_r, dst, offs, out):
             for a in range(BLOCKS):
                 nc.tensor.transpose(flipped[:, a, :], wmu_blocks[:, a, :], identity[:])
             for a in range(BLOCKS):
-                nc.tensor.matmul(scores[:, a : a + 1], wmu_bf_blocks[:, a, :], attn_l_bf[:], start=True, stop=True)
+                nc.tensor.matmul(scores[:, a : a + 1], wmu_bf_blocks[:, a, :], attn_l_bf, start=True, stop=True)
             flipped_of.append(flipped)
             scores_of.append(scores)
 
@@ -144,22 +150,23 @@ def tile_gatedge_kernel(tc, x, edge, w_edge, attn_l, attn_r, dst, offs, out):
             nc.vector.tensor_tensor(weights[:, group, 0:BLOCKS], p_pos[:, group, :], p_neg[:, group, :], ALU.max)
             nc.vector.tensor_reduce(row_sum[:, group], weights[:, group, :], AXIS.X, ALU.add)
             nc.tensor.matmul(den_ps[:, group], same_machine[:], row_sum[:, group], start=True, stop=True)
-            for a in range(BLOCKS):
-                for r in range(first, first + count):
-                    nc.vector.scalar_tensor_tensor(
-                        acc_of[r][:], flipped_of[r][:, a, :], weights[:, r, a : a + 1], acc_of[r][:], ALU.mult, ALU.add
-                    )
+            def add_blocks(blocks):
+                for a in blocks:
+                    for r in range(first, first + count):
+                        nc.vector.scalar_tensor_tensor(
+                            acc_of[r][:], flipped_of[r][:, a, :], weights[:, r, a : a + 1], acc_of[r][:], ALU.mult, ALU.add
+                        )
+
+            add_blocks(range(0, BLOCKS // 2))
             nc.vector.reciprocal(rden[:, group], den_ps[:, group])
-            nc.vector.tensor_tensor(
-                fold[:, group, :],
-                row_of_machine.unsqueeze(1).to_broadcast([ROWS, count, MACH]),
-                rden[:, group].unsqueeze(2).to_broadcast([ROWS, count, MACH]),
-                ALU.mult,
-            )
+            for r in range(first, first + count):
+                nc.scalar.activation(fold[:, r, :], row_of_machine, FUNC.Copy, scale=rden[:, r : r + 1])
+            add_blocks(range(BLOCKS // 2, BLOCKS))
             for r in range(first, first + count):
                 nc.tensor.matmul(z_ps[:, r * MACH : (r + 1) * MACH], acc_of[r][:], fold[:, r, :], start=True, stop=True)
 
         scale_edge(0)
+        nc.scalar.copy(attn_bf[:], attn_ps[:])
         scale_edge(1)
         own_scores()
         scale_edge(2)
@@ -177,6 +184,7 @@ def tile_gatedge_kernel(tc, x, edge, w_edge, attn_l, attn_r, dst, offs, out):
         look_up(3)
         exponentials(2)
         exponentials(3)
+        nc.scalar.activation(scratch[:], scratch[:], FUNC.Sigmoid)
         weigh(0, 2)
         weigh(2, 2)
 

@@ -13,12 +13,14 @@ S = 1024
 N = 2048
 M = 128
 E = 16
+PER_COLUMN = 16
 PIECE = 512
 N_PIECES = N // PIECE
 MACH = PIECE // E
 ROWS = 128
 BLOCKS = PIECE // ROWS
 SHARE = ROWS // MACH
+PAIR = 2
 SLOPE = 0.2
 
 FLOPS = 2 * C * N + 2 * C * M + 2 * C * N
@@ -30,14 +32,17 @@ def tile_gatedge_kernel(tc, x, edge, w_edge, attn_l, attn_r, dst, offs, out):
         tc.tile_pool(name="held", bufs=1) as held,
         tc.tile_pool(name="pieces", bufs=N_PIECES) as pieces,
         tc.psum_pool(name="flip_banks", bufs=N_PIECES) as flip_banks,
-        tc.psum_pool(name="score_banks", bufs=2) as score_banks,
+        tc.psum_pool(name="column_banks", bufs=2) as column_banks,
         tc.psum_pool(name="single_banks", bufs=1) as single_banks,
     ):
         vector_rows = held.tile([1, 3 * C], F32, name="vector_rows")
-        nc.scalar.dma_start(vector_rows[:, 0:C], w_edge.rearrange("c one -> one c"))
+        w_edge_row = vector_rows[:, 0:C]
+        attn_r_row = vector_rows[:, C : 2 * C]
+        attn_l_row = vector_rows[:, 2 * C : 3 * C]
+        nc.scalar.dma_start(w_edge_row, w_edge.rearrange("c one -> one c"))
         table = held.tile([C, S], F32, name="table")
         nc.sync.dma_start(table[:], x)
-        offsets = held.tile([C, N // 16], U16, name="offsets")
+        offsets = held.tile([C, N // PER_COLUMN], U16, name="offsets")
         nc.sync.dma_start(offsets[:], offs)
         edge_all = held.tile([C, N], F32, name="edge_all")
         nc.scalar.dma_start(edge_all[:, 0:PIECE], edge[0, 0:PIECE].partition_broadcast(C))
@@ -46,8 +51,8 @@ def tile_gatedge_kernel(tc, x, edge, w_edge, attn_l, attn_r, dst, offs, out):
         nc.scalar.activation(scratch[:], scratch[:], FUNC.Exp)
         dst_f32 = held.tile([C, M], F32, name="dst_f32")
         nc.scalar.dma_start(dst_f32[:], dst)
-        nc.sync.dma_start(vector_rows[:, C : 2 * C], attn_r.rearrange("c one -> one c"))
-        nc.sync.dma_start(vector_rows[:, 2 * C : 3 * C], attn_l.rearrange("c one -> one c"))
+        nc.sync.dma_start(attn_r_row, attn_r.rearrange("c one -> one c"))
+        nc.sync.dma_start(attn_l_row, attn_l.rearrange("c one -> one c"))
         nc.scalar.dma_start(edge_all[:, PIECE:N], edge[0, PIECE:N].partition_broadcast(C))
 
         identity = held.tile([C, C], F32, name="identity")
@@ -58,135 +63,106 @@ def tile_gatedge_kernel(tc, x, edge, w_edge, attn_l, attn_r, dst, offs, out):
 
         one = held.tile([1, 1], F32, name="one")
         nc.vector.memset(one[:], 1.0)
-        w_edge_ps = score_banks.tile([C, 1], F32, name="w_edge_ps", tag="scores")
-        nc.tensor.matmul(w_edge_ps[:], vector_rows[:, 0:C], one[:], start=True, stop=True)
+        w_edge_ps = column_banks.tile([C, 1], F32, name="w_edge_ps", tag="columns")
+        nc.tensor.matmul(w_edge_ps[:], w_edge_row, one[:], start=True, stop=True)
         w_edge_col = held.tile([C, 1], F32, name="w_edge_col")
         nc.vector.tensor_copy(w_edge_col[:], w_edge_ps[:])
-        attn_ps = score_banks.tile([C, 2], F32, name="attn_ps", tag="scores")
-        for k in range(2):
-            nc.tensor.matmul(attn_ps[:, k : k + 1], vector_rows[:, (k + 1) * C : (k + 2) * C], one[:], start=True, stop=True)
+        attn_ps = column_banks.tile([C, 2], F32, name="attn_ps", tag="columns")
+        nc.tensor.matmul(attn_ps[:, 0:1], attn_r_row, one[:], start=True, stop=True)
+        nc.tensor.matmul(attn_ps[:, 1:2], attn_l_row, one[:], start=True, stop=True)
         attn_bf = held.tile([C, 2], BF16, name="attn_bf")
+        nc.scalar.copy(attn_bf[:], attn_ps[:])
         attn_r_bf = attn_bf[:, 0:1]
         attn_l_bf = attn_bf[:, 1:2]
 
-        er = held.tile([ROWS, N_PIECES], F32, name="er")
-        er_slope = held.tile([ROWS, N_PIECES], F32, name="er_slope")
-        p_pos = held.tile([ROWS, N_PIECES, BLOCKS], F32, name="p_pos")
-        p_neg = held.tile([ROWS, N_PIECES, BLOCKS], F32, name="p_neg")
-        weights = held.tile([ROWS, N_PIECES, BLOCKS + 1], F32, name="weights")
-        row_sum = held.tile([ROWS, N_PIECES], F32, name="row_sum")
-        rden = held.tile([ROWS, N_PIECES], F32, name="rden")
-        fold = held.tile([ROWS, N_PIECES, MACH], F32, name="fold")
-        den_ps = single_banks.tile([ROWS, N_PIECES], F32, name="den_ps")
-        z_ps = single_banks.tile([C, M], F32, name="z_ps")
-        dst_flipped = flip_banks.tile([ROWS, N_PIECES, C], F32, name="dst_flipped", tag="flipped")
-        pkk_pos = held.tile([ROWS, N_PIECES], F32, name="pkk_pos")
-        pkk_neg = held.tile([ROWS, N_PIECES], F32, name="pkk_neg")
         we_of = []
-        acc_of = []
-        flipped_of = []
-        scores_of = []
-
-        def scale_edge(r):
+        for r in range(N_PIECES):
             we = pieces.tile([C, PIECE], F32, name="we")
             nc.scalar.activation(
                 we[:], edge_all[:, r * PIECE : (r + 1) * PIECE], FUNC.Copy, scale=w_edge_col[:, 0:1]
             )
             we_of.append(we)
 
-        def own_scores():
-            dst_wide = dst_f32[:].unsqueeze(2).to_broadcast([C, M, SHARE])
-            dst_rep_bf = held.tile([C, M, SHARE], BF16, name="dst_rep_bf")
-            nc.vector.tensor_copy(dst_rep_bf[:], dst_wide)
-            dst_rep = held.tile([C, M, SHARE], F32, name="dst_rep")
-            nc.vector.tensor_copy(dst_rep[:], dst_wide)
-            dst_rep_bf_blocks = dst_rep_bf[:].rearrange("c m u -> c (m u)")
-            dst_rep_blocks = dst_rep[:].rearrange("c m u -> c (m u)")
-            er_ps = score_banks.tile([ROWS, N_PIECES], F32, name="er_ps", tag="scores")
-            for r in range(N_PIECES):
-                rows = slice(r * ROWS, (r + 1) * ROWS)
-                nc.tensor.matmul(er_ps[:, r : r + 1], dst_rep_bf_blocks[:, rows], attn_r_bf, start=True, stop=True)
-            for r in range(N_PIECES):
-                rows = slice(r * ROWS, (r + 1) * ROWS)
-                nc.tensor.transpose(dst_flipped[:, r, :], dst_rep_blocks[:, rows], identity[:])
-            nc.scalar.copy(er[:], er_ps[:])
-            nc.scalar.mul(er_slope[:], er_ps[:], SLOPE)
-            nc.scalar.activation(pkk_pos[:], er_ps[:], FUNC.Exp, scale=2.0)
-            nc.scalar.activation(pkk_neg[:], er_ps[:], FUNC.Exp, scale=2.0 * SLOPE)
-
-        def own_weights():
-            pkk = held.tile([ROWS, N_PIECES], F32, name="pkk")
-            nc.vector.tensor_tensor(pkk[:], pkk_pos[:], pkk_neg[:], ALU.max)
-            nc.vector.tensor_scalar(weights[:, :, BLOCKS], pkk[:], 1.0 / SHARE, None, ALU.mult)
-
-        def own_rows(r):
+        dst_wide = dst_f32[:].unsqueeze(2).to_broadcast([C, M, SHARE])
+        dst_rep_bf = held.tile([C, M, SHARE], BF16, name="dst_rep_bf")
+        nc.vector.tensor_copy(dst_rep_bf[:], dst_wide)
+        dst_rep = held.tile([C, M, SHARE], F32, name="dst_rep")
+        nc.vector.tensor_copy(dst_rep[:], dst_wide)
+        dst_rep_bf_blocks = dst_rep_bf[:].rearrange("c m u -> c (m u)")
+        dst_rep_blocks = dst_rep[:].rearrange("c m u -> c (m u)")
+        er_ps = column_banks.tile([ROWS, N_PIECES], F32, name="er_ps", tag="columns")
+        dst_flipped = flip_banks.tile([ROWS, N_PIECES, C], F32, name="dst_flipped", tag="flipped")
+        for r in range(N_PIECES):
+            rows = slice(r * ROWS, (r + 1) * ROWS)
+            nc.tensor.matmul(er_ps[:, r : r + 1], dst_rep_bf_blocks[:, rows], attn_r_bf, start=True, stop=True)
+        for r in range(N_PIECES):
+            rows = slice(r * ROWS, (r + 1) * ROWS)
+            nc.tensor.transpose(dst_flipped[:, r, :], dst_rep_blocks[:, rows], identity[:])
+        er = held.tile([ROWS, N_PIECES], F32, name="er")
+        nc.scalar.copy(er[:], er_ps[:])
+        er_slope = held.tile([ROWS, N_PIECES], F32, name="er_slope")
+        nc.scalar.mul(er_slope[:], er_ps[:], SLOPE)
+        pkk_pos = held.tile([ROWS, N_PIECES], F32, name="pkk_pos")
+        nc.scalar.activation(pkk_pos[:], er_ps[:], FUNC.Exp, scale=2.0)
+        pkk_neg = held.tile([ROWS, N_PIECES], F32, name="pkk_neg")
+        nc.scalar.activation(pkk_neg[:], er_ps[:], FUNC.Exp, scale=2.0 * SLOPE)
+        pkk = held.tile([ROWS, N_PIECES], F32, name="pkk")
+        nc.vector.tensor_tensor(pkk[:], pkk_pos[:], pkk_neg[:], ALU.max)
+        weights = held.tile([ROWS, N_PIECES, BLOCKS + 1], F32, name="weights")
+        nc.vector.tensor_scalar(weights[:, :, BLOCKS], pkk[:], 1.0 / SHARE, None, ALU.mult)
+        acc_of = []
+        for r in range(N_PIECES):
             acc = pieces.tile([ROWS, C], F32, name="acc")
             nc.scalar.activation(acc[:], dst_flipped[:, r, :], FUNC.Copy, scale=weights[:, r, BLOCKS : BLOCKS + 1])
             acc_of.append(acc)
 
-        def look_up(r):
+        p_pos = held.tile([ROWS, N_PIECES, BLOCKS], F32, name="p_pos")
+        p_neg = held.tile([ROWS, N_PIECES, BLOCKS], F32, name="p_neg")
+        flipped_of = []
+        for r in range(N_PIECES):
             wmu = pieces.tile([C, PIECE], F32, name="wmu")
-            picked = table[:].indirect(offsets[:, r * (PIECE // 16) : (r + 1) * (PIECE // 16)])
+            picked = table[:].indirect(offsets[:, r * (PIECE // PER_COLUMN) : (r + 1) * (PIECE // PER_COLUMN)])
             nc.vector.tensor_tensor(wmu[:], picked, we_of[r][:], ALU.add)
             wmu_bf = pieces.tile([C, PIECE], BF16, name="wmu_bf")
             nc.scalar.copy(wmu_bf[:], wmu[:])
             wmu_blocks = wmu[:].rearrange("c (i a) -> c a i", a=BLOCKS)
             wmu_bf_blocks = wmu_bf[:].rearrange("c (i a) -> c a i", a=BLOCKS)
             flipped = flip_banks.tile([ROWS, BLOCKS, C], F32, name="flipped", tag="flipped")
-            scores = score_banks.tile([ROWS, BLOCKS], F32, name="scores", tag="scores")
             for a in range(BLOCKS):
                 nc.tensor.transpose(flipped[:, a, :], wmu_blocks[:, a, :], identity[:])
-            for a in range(BLOCKS):
-                nc.tensor.matmul(scores[:, a : a + 1], wmu_bf_blocks[:, a, :], attn_l_bf, start=True, stop=True)
             flipped_of.append(flipped)
-            scores_of.append(scores)
+            s_ps = column_banks.tile([ROWS, BLOCKS], F32, name="s_ps", tag="columns")
+            for a in range(BLOCKS):
+                nc.tensor.matmul(s_ps[:, a : a + 1], wmu_bf_blocks[:, a, :], attn_l_bf, start=True, stop=True)
+            nc.scalar.activation(p_pos[:, r, :], s_ps[:], FUNC.Exp, bias=er[:, r : r + 1], scale=1.0)
+            nc.scalar.activation(p_neg[:, r, :], s_ps[:], FUNC.Exp, bias=er_slope[:, r : r + 1], scale=SLOPE)
 
-        def exponentials(r):
-            nc.scalar.activation(p_pos[:, r, :], scores_of[r][:], FUNC.Exp, bias=er[:, r : r + 1], scale=1.0)
-            nc.scalar.activation(p_neg[:, r, :], scores_of[r][:], FUNC.Exp, bias=er_slope[:, r : r + 1], scale=SLOPE)
+        row_sum = held.tile([ROWS, N_PIECES], F32, name="row_sum")
+        rden = held.tile([ROWS, N_PIECES], F32, name="rden")
+        fold = held.tile([ROWS, N_PIECES, MACH], F32, name="fold")
+        den_ps = single_banks.tile([ROWS, N_PIECES], F32, name="den_ps")
+        z_ps = single_banks.tile([C, M], F32, name="z_ps")
 
-        def weigh(first, count):
-            group = slice(first, first + count)
-            nc.vector.tensor_tensor(weights[:, group, 0:BLOCKS], p_pos[:, group, :], p_neg[:, group, :], ALU.max)
-            nc.vector.tensor_reduce(row_sum[:, group], weights[:, group, :], AXIS.X, ALU.add)
-            nc.tensor.matmul(den_ps[:, group], same_machine[:], row_sum[:, group], start=True, stop=True)
-            def add_blocks(blocks):
-                for a in blocks:
-                    for r in range(first, first + count):
-                        nc.vector.scalar_tensor_tensor(
-                            acc_of[r][:], flipped_of[r][:, a, :], weights[:, r, a : a + 1], acc_of[r][:], ALU.mult, ALU.add
-                        )
+        def add_blocks(pair, blocks):
+            for a in blocks:
+                for r in pair:
+                    nc.vector.scalar_tensor_tensor(
+                        acc_of[r][:], flipped_of[r][:, a, :], weights[:, r, a : a + 1], acc_of[r][:], ALU.mult, ALU.add
+                    )
 
-            add_blocks(range(0, BLOCKS // 2))
-            nc.vector.reciprocal(rden[:, group], den_ps[:, group])
-            for r in range(first, first + count):
+        for first in range(0, N_PIECES, PAIR):
+            pair = range(first, first + PAIR)
+            both = slice(first, first + PAIR)
+            nc.vector.tensor_tensor(weights[:, both, 0:BLOCKS], p_pos[:, both, :], p_neg[:, both, :], ALU.max)
+            nc.vector.tensor_reduce(row_sum[:, both], weights[:, both, :], AXIS.X, ALU.add)
+            nc.tensor.matmul(den_ps[:, both], same_machine[:], row_sum[:, both], start=True, stop=True)
+            add_blocks(pair, range(0, BLOCKS // 2))
+            nc.vector.reciprocal(rden[:, both], den_ps[:, both])
+            for r in pair:
                 nc.scalar.activation(fold[:, r, :], row_of_machine, FUNC.Copy, scale=rden[:, r : r + 1])
-            add_blocks(range(BLOCKS // 2, BLOCKS))
-            for r in range(first, first + count):
+            add_blocks(pair, range(BLOCKS // 2, BLOCKS))
+            for r in pair:
                 nc.tensor.matmul(z_ps[:, r * MACH : (r + 1) * MACH], acc_of[r][:], fold[:, r, :], start=True, stop=True)
-
-        scale_edge(0)
-        nc.scalar.copy(attn_bf[:], attn_ps[:])
-        scale_edge(1)
-        own_scores()
-        scale_edge(2)
-        look_up(0)
-        own_weights()
-        scale_edge(3)
-        own_rows(0)
-        own_rows(1)
-        look_up(1)
-        exponentials(0)
-        own_rows(2)
-        own_rows(3)
-        look_up(2)
-        exponentials(1)
-        look_up(3)
-        exponentials(2)
-        exponentials(3)
-        nc.scalar.activation(scratch[:], scratch[:], FUNC.Sigmoid)
-        weigh(0, 2)
-        weigh(2, 2)
 
         result = held.tile([C, M], F32, name="result")
         nc.scalar.activation(result[:], z_ps[:], FUNC.Sigmoid)

@@ -20,7 +20,7 @@ MACH = PIECE // E
 ROWS = 128
 BLOCKS = PIECE // ROWS
 SHARE = ROWS // MACH
-PAIR = 2
+PAIR = 4
 SLOPE = 0.2
 
 FLOPS = 2 * C * N + 2 * C * M + 2 * C * N

@@ -46,14 +46,14 @@ def tile_gatedge_kernel(tc, x, edge, w_edge, attn_l, attn_r, dst, offs, out):
         nc.sync.dma_start(offsets[:], offs)
         edge_all = held.tile([C, N], F32, name="edge_all")
         nc.scalar.dma_start(edge_all[:, 0:PIECE], edge[0, 0:PIECE].partition_broadcast(C))
+        nc.scalar.dma_start(edge_all[:, PIECE:N], edge[0, PIECE:N].partition_broadcast(C))
+        dst_f32 = held.tile([C, M], F32, name="dst_f32")
+        nc.sync.dma_start(dst_f32[:], dst)
+        nc.sync.dma_start(attn_r_row, attn_r.rearrange("c one -> one c"))
+        nc.sync.dma_start(attn_l_row, attn_l.rearrange("c one -> one c"))
         scratch = held.tile([C, 1], F32, name="scratch")
         nc.gpsimd.memset(scratch[:], 0.0)
         nc.scalar.activation(scratch[:], scratch[:], FUNC.Exp)
-        dst_f32 = held.tile([C, M], F32, name="dst_f32")
-        nc.scalar.dma_start(dst_f32[:], dst)
-        nc.sync.dma_start(attn_r_row, attn_r.rearrange("c one -> one c"))
-        nc.sync.dma_start(attn_l_row, attn_l.rearrange("c one -> one c"))
-        nc.scalar.dma_start(edge_all[:, PIECE:N], edge[0, PIECE:N].partition_broadcast(C))
 
         identity = held.tile([C, C], F32, name="identity")
         make_identity(nc, identity[:])

@@ -1,5 +1,4 @@
 import concourse.mybir as mybir
-from concourse.masks import make_block_diagonal, make_identity
 
 F32 = mybir.dt.float32
 BF16 = mybir.dt.bfloat16
@@ -52,17 +51,31 @@ def tile_gatedge_kernel(tc, x, edge, w_edge, attn_l, attn_r, dst, offs, out):
         nc.sync.dma_start(attn_r_row, attn_r.rearrange("c one -> one c"))
         nc.sync.dma_start(attn_l_row, attn_l.rearrange("c one -> one c"))
         scratch = held.tile([C, 1], F32, name="scratch")
-        nc.gpsimd.memset(scratch[:], 0.0)
+        nc.vector.memset(scratch[:], 0.0)
         nc.scalar.activation(scratch[:], scratch[:], FUNC.Exp)
-
-        identity = held.tile([C, C], F32, name="identity")
-        make_identity(nc, identity[:])
-        same_machine = held.tile([ROWS, ROWS], F32, name="same_machine")
-        make_block_diagonal(nc, same_machine[:], SHARE)
-        row_of_machine = same_machine[:].rearrange("i (m u) -> i u m", u=SHARE)[:, 0, :]
 
         one = held.tile([1, 1], F32, name="one")
         nc.vector.memset(one[:], 1.0)
+        all_ones = held.tile([C, C], F32, name="all_ones")
+        nc.vector.memset(all_ones[:], 1.0)
+        first_of_machine = held.tile([ROWS, MACH, SHARE], F32, name="first_of_machine")
+        nc.vector.memset(first_of_machine[:], 0.0)
+        nc.vector.memset(first_of_machine[:, :, 0], 1.0)
+        column_number = held.tile([C, C], F32, name="column_number")
+        nc.vector.tensor_tensor_scan(column_number[:], all_ones[:], all_ones[:], 0.0, ALU.mult, ALU.add)
+        column_machine = held.tile([ROWS, ROWS], F32, name="column_machine")
+        nc.vector.tensor_tensor_scan(
+            column_machine[:], all_ones[:], first_of_machine[:].rearrange("i m u -> i (m u)"), 0.0, ALU.mult, ALU.add
+        )
+        partition_ps = column_banks.tile([C, 2], F32, name="partition_ps", tag="columns")
+        nc.tensor.matmul(partition_ps[:, 0:1], column_number[0:1, :], one[:], start=True, stop=True)
+        nc.tensor.matmul(partition_ps[:, 1:2], column_machine[0:1, :], one[:], start=True, stop=True)
+        identity = held.tile([C, C], F32, name="identity")
+        nc.vector.tensor_scalar(identity[:], column_number[:], partition_ps[:, 0:1], None, ALU.is_equal)
+        same_machine = held.tile([ROWS, ROWS], F32, name="same_machine")
+        nc.vector.tensor_scalar(same_machine[:], column_machine[:], partition_ps[:, 1:2], None, ALU.is_equal)
+        row_of_machine = same_machine[:].rearrange("i (m u) -> i u m", u=SHARE)[:, 0, :]
+
         w_edge_ps = column_banks.tile([C, 1], F32, name="w_edge_ps", tag="columns")
         nc.tensor.matmul(w_edge_ps[:], w_edge_row, one[:], start=True, stop=True)
         w_edge_col = held.tile([C, 1], F32, name="w_edge_col")

@@ -19,7 +19,7 @@ MACH = PIECE // E
 ROWS = 128
 BLOCKS = PIECE // ROWS
 SHARE = ROWS // MACH
-PAIR = 4
+PAIR = 2
 SLOPE = 0.2
 
 FLOPS = 2 * C * N + 2 * C * M + 2 * C * N

@@ -136,10 +136,9 @@ def tile_gatedge_kernel(tc, x, edge, w_edge, attn_l, attn_r, dst, offs, out):
             wmu = pieces.tile([C, PIECE], F32, name="wmu")
             picked = table[:].indirect(offsets[:, r * (PIECE // PER_COLUMN) : (r + 1) * (PIECE // PER_COLUMN)])
             nc.vector.tensor_tensor(wmu[:], picked, we_of[r][:], ALU.add)
-            wmu_bf = pieces.tile([C, PIECE], BF16, name="wmu_bf")
-            nc.scalar.copy(wmu_bf[:], wmu[:])
             wmu_blocks = wmu[:].rearrange("c (i a) -> c a i", a=BLOCKS)
-            wmu_bf_blocks = wmu_bf[:].rearrange("c (i a) -> c a i", a=BLOCKS)
+            wmu_bf_blocks = pieces.tile([C, BLOCKS, ROWS], BF16, name="wmu_bf_blocks")
+            nc.scalar.copy(wmu_bf_blocks[:].rearrange("c a i -> c i a"), wmu[:].rearrange("c (i a) -> c i a", a=BLOCKS))
             flipped = flip_banks.tile([ROWS, BLOCKS, C], F32, name="flipped", tag="flipped")
             for a in range(BLOCKS):
                 nc.tensor.transpose(flipped[:, a, :], wmu_blocks[:, a, :], identity[:])

@@ -1,3 +1,5 @@
+import math
+
 import concourse.mybir as mybir
 
 F32 = mybir.dt.float32
@@ -21,6 +23,7 @@ BLOCKS = PIECE // ROWS
 SHARE = ROWS // MACH
 PAIR = 2
 SLOPE = 0.2
+LOG_SHARE_OF_ROW = -math.log(SHARE)
 
 FLOPS = 2 * C * N + 2 * C * M + 2 * C * N
 
@@ -116,13 +119,11 @@ def tile_gatedge_kernel(tc, x, edge, w_edge, attn_l, attn_r, dst, offs, out):
         er_slope = held.tile([ROWS, N_PIECES], F32, name="er_slope")
         nc.scalar.mul(er_slope[:], er_ps[:], SLOPE)
         pkk_pos = held.tile([ROWS, N_PIECES], F32, name="pkk_pos")
-        nc.scalar.activation(pkk_pos[:], er_ps[:], FUNC.Exp, scale=2.0)
+        nc.scalar.activation(pkk_pos[:], er_ps[:], FUNC.Exp, bias=LOG_SHARE_OF_ROW, scale=2.0)
         pkk_neg = held.tile([ROWS, N_PIECES], F32, name="pkk_neg")
-        nc.scalar.activation(pkk_neg[:], er_ps[:], FUNC.Exp, scale=2.0 * SLOPE)
-        pkk = held.tile([ROWS, N_PIECES], F32, name="pkk")
-        nc.vector.tensor_tensor(pkk[:], pkk_pos[:], pkk_neg[:], ALU.max)
+        nc.scalar.activation(pkk_neg[:], er_ps[:], FUNC.Exp, bias=LOG_SHARE_OF_ROW, scale=2.0 * SLOPE)
         weights = held.tile([ROWS, N_PIECES, BLOCKS + 1], F32, name="weights")
-        nc.vector.tensor_scalar(weights[:, :, BLOCKS], pkk[:], 1.0 / SHARE, None, ALU.mult)
+        nc.vector.tensor_tensor(weights[:, :, BLOCKS], pkk_pos[:], pkk_neg[:], ALU.max)
         acc_of = []
         for r in range(N_PIECES):
             acc = pieces.tile([ROWS, C], F32, name="acc")

@@ -47,8 +47,7 @@ def tile_gatedge_kernel(tc, x, edge, w_edge, attn_l, attn_r, dst, offs, out):
         offsets = held.tile([C, N // PER_COLUMN], U16, name="offsets")
         nc.sync.dma_start(offsets[:], offs)
         edge_all = held.tile([C, N], F32, name="edge_all")
-        nc.scalar.dma_start(edge_all[:, 0:PIECE], edge[0, 0:PIECE].partition_broadcast(C))
-        nc.scalar.dma_start(edge_all[:, PIECE:N], edge[0, PIECE:N].partition_broadcast(C))
+        nc.scalar.dma_start(edge_all[:], edge[0, :].partition_broadcast(C))
         dst_f32 = held.tile([C, M], F32, name="dst_f32")
         nc.sync.dma_start(dst_f32[:], dst)
         nc.sync.dma_start(attn_r_row, attn_r.rearrange("c one -> one c"))

@@ -47,7 +47,9 @@ def tile_gatedge_kernel(tc, x, edge, w_edge, attn_l, attn_r, dst, offs, out):
         offsets = held.tile([C, N // PER_COLUMN], U16, name="offsets")
         nc.sync.dma_start(offsets[:], offs)
         edge_all = held.tile([C, N], F32, name="edge_all")
-        nc.scalar.dma_start(edge_all[:], edge[0, :].partition_broadcast(C))
+        half = N // 2
+        nc.scalar.dma_start(edge_all[:, 0:half], edge[0, 0:half].partition_broadcast(C))
+        nc.scalar.dma_start(edge_all[:, half:N], edge[0, half:N].partition_broadcast(C))
         dst_f32 = held.tile([C, M], F32, name="dst_f32")
         nc.sync.dma_start(dst_f32[:], dst)
         nc.sync.dma_start(attn_r_row, attn_r.rearrange("c one -> one c"))

@@ -33,15 +33,12 @@ def tile_gatedge_kernel(tc, x, edge, w_edge, attn_l, attn_r, dst, offs, out):
     with (
         tc.tile_pool(name="held", bufs=1) as held,
         tc.tile_pool(name="pieces", bufs=N_PIECES) as pieces,
-        tc.psum_pool(name="flip_banks", bufs=N_PIECES) as flip_banks,
+        tc.psum_pool(name="flip_banks", bufs=N_PIECES + 1) as flip_banks,
         tc.psum_pool(name="column_banks", bufs=2) as column_banks,
-        tc.psum_pool(name="single_banks", bufs=1) as single_banks,
+        tc.psum_pool(name="z_bank", bufs=1) as z_bank,
     ):
-        vector_rows = held.tile([1, 3 * C], F32, name="vector_rows")
-        w_edge_row = vector_rows[:, 0:C]
-        attn_r_row = vector_rows[:, C : 2 * C]
-        attn_l_row = vector_rows[:, 2 * C : 3 * C]
-        nc.scalar.dma_start(w_edge_row, w_edge.rearrange("c one -> one c"))
+        w_edge_col = held.tile([C, 1], F32, name="w_edge_col")
+        nc.scalar.dma_start(w_edge_col[:], w_edge)
         table = held.tile([C, S], F32, name="table")
         nc.sync.dma_start(table[:], x)
         offsets = held.tile([C, N // PER_COLUMN], U16, name="offsets")
@@ -49,11 +46,13 @@ def tile_gatedge_kernel(tc, x, edge, w_edge, attn_l, attn_r, dst, offs, out):
         edge_all = held.tile([C, N], F32, name="edge_all")
         half = N // 2
         nc.scalar.dma_start(edge_all[:, 0:half], edge[0, 0:half].partition_broadcast(C))
+        attn_l_col = held.tile([C, 1], F32, name="attn_l_col")
+        nc.scalar.dma_start(attn_l_col[:], attn_l)
         nc.scalar.dma_start(edge_all[:, half:N], edge[0, half:N].partition_broadcast(C))
         dst_f32 = held.tile([C, M], F32, name="dst_f32")
         nc.sync.dma_start(dst_f32[:], dst)
-        nc.sync.dma_start(attn_r_row, attn_r.rearrange("c one -> one c"))
-        nc.sync.dma_start(attn_l_row, attn_l.rearrange("c one -> one c"))
+        attn_r_col = held.tile([C, 1], F32, name="attn_r_col")
+        nc.sync.dma_start(attn_r_col[:], attn_r)
         scratch = held.tile([C, 1], F32, name="scratch")
         nc.vector.memset(scratch[:], 0.0)
         nc.scalar.activation(scratch[:], scratch[:], FUNC.Exp)
@@ -80,17 +79,11 @@ def tile_gatedge_kernel(tc, x, edge, w_edge, attn_l, attn_r, dst, offs, out):
         nc.vector.tensor_scalar(same_machine[:], column_machine[:], partition_ps[:, 1:2], None, ALU.is_equal)
         row_of_machine = same_machine[:].rearrange("i (m u) -> i u m", u=SHARE)[:, 0, :]
 
-        w_edge_ps = column_banks.tile([C, 1], F32, name="w_edge_ps", tag="columns")
-        nc.tensor.matmul(w_edge_ps[:], w_edge_row, one[:], start=True, stop=True)
-        w_edge_col = held.tile([C, 1], F32, name="w_edge_col")
-        nc.vector.tensor_copy(w_edge_col[:], w_edge_ps[:])
-        attn_ps = column_banks.tile([C, 2], F32, name="attn_ps", tag="columns")
-        nc.tensor.matmul(attn_ps[:, 0:1], attn_r_row, one[:], start=True, stop=True)
-        nc.tensor.matmul(attn_ps[:, 1:2], attn_l_row, one[:], start=True, stop=True)
         attn_bf = held.tile([C, 2], BF16, name="attn_bf")
-        nc.scalar.copy(attn_bf[:], attn_ps[:])
         attn_r_bf = attn_bf[:, 0:1]
         attn_l_bf = attn_bf[:, 1:2]
+        nc.gpsimd.tensor_copy(attn_r_bf, attn_r_col[:])
+        nc.gpsimd.tensor_copy(attn_l_bf, attn_l_col[:])
 
         we_of = []
         for r in range(N_PIECES):
@@ -119,16 +112,17 @@ def tile_gatedge_kernel(tc, x, edge, w_edge, attn_l, attn_r, dst, offs, out):
         nc.scalar.copy(er[:], er_ps[:])
         er_slope = held.tile([ROWS, N_PIECES], F32, name="er_slope")
         nc.scalar.mul(er_slope[:], er_ps[:], SLOPE)
-        pkk_pos = held.tile([ROWS, N_PIECES], F32, name="pkk_pos")
-        nc.scalar.activation(pkk_pos[:], er_ps[:], FUNC.Exp, bias=LOG_SHARE_OF_ROW, scale=2.0)
-        pkk_neg = held.tile([ROWS, N_PIECES], F32, name="pkk_neg")
-        nc.scalar.activation(pkk_neg[:], er_ps[:], FUNC.Exp, bias=LOG_SHARE_OF_ROW, scale=2.0 * SLOPE)
         weights = held.tile([ROWS, N_PIECES, BLOCKS + 1], F32, name="weights")
-        nc.vector.tensor_tensor(weights[:, :, BLOCKS], pkk_pos[:], pkk_neg[:], ALU.max)
+        er_relu = held.tile([ROWS, N_PIECES], F32, name="er_relu")
+        nc.scalar.activation(er_relu[:], er_ps[:], FUNC.Relu, scale=2.0 * (1.0 - SLOPE))
+        er_shifted = held.tile([ROWS, N_PIECES], F32, name="er_shifted")
+        nc.scalar.add(er_shifted[:], er_ps[:], LOG_SHARE_OF_ROW / (2.0 * SLOPE))
         acc_of = []
         for r in range(N_PIECES):
+            own_weight = weights[:, r, BLOCKS : BLOCKS + 1]
+            nc.scalar.activation(own_weight, er_shifted[:, r : r + 1], FUNC.Exp, bias=er_relu[:, r : r + 1], scale=2.0 * SLOPE)
             acc = pieces.tile([ROWS, C], F32, name="acc")
-            nc.scalar.activation(acc[:], dst_flipped[:, r, :], FUNC.Copy, scale=weights[:, r, BLOCKS : BLOCKS + 1])
+            nc.scalar.activation(acc[:], dst_flipped[:, r, :], FUNC.Copy, scale=own_weight)
             acc_of.append(acc)
 
         p_pos = held.tile([ROWS, N_PIECES, BLOCKS], F32, name="p_pos")
@@ -139,8 +133,12 @@ def tile_gatedge_kernel(tc, x, edge, w_edge, attn_l, attn_r, dst, offs, out):
             picked = table[:].indirect(offsets[:, r * (PIECE // PER_COLUMN) : (r + 1) * (PIECE // PER_COLUMN)])
             nc.vector.tensor_tensor(wmu[:], picked, we_of[r][:], ALU.add)
             wmu_blocks = wmu[:].rearrange("c (i a) -> c a i", a=BLOCKS)
-            wmu_bf_blocks = pieces.tile([C, BLOCKS, ROWS], BF16, name="wmu_bf_blocks")
-            nc.scalar.copy(wmu_bf_blocks[:].rearrange("c a i -> c i a"), wmu[:].rearrange("c (i a) -> c i a", a=BLOCKS))
+            wmu_bf = pieces.tile([C, PIECE], BF16, name="wmu_bf")
+            if r == N_PIECES - 1:
+                nc.vector.tensor_copy(wmu_bf[:], wmu[:])
+            else:
+                nc.scalar.copy(wmu_bf[:], wmu[:])
+            wmu_bf_blocks = wmu_bf[:].rearrange("c (i a) -> c a i", a=BLOCKS)
             flipped = flip_banks.tile([ROWS, BLOCKS, C], F32, name="flipped", tag="flipped")
             for a in range(BLOCKS):
                 nc.tensor.transpose(flipped[:, a, :], wmu_blocks[:, a, :], identity[:])
@@ -154,8 +152,7 @@ def tile_gatedge_kernel(tc, x, edge, w_edge, attn_l, attn_r, dst, offs, out):
         row_sum = held.tile([ROWS, N_PIECES], F32, name="row_sum")
         rden = held.tile([ROWS, N_PIECES], F32, name="rden")
         fold = held.tile([ROWS, N_PIECES, MACH], F32, name="fold")
-        den_ps = single_banks.tile([ROWS, N_PIECES], F32, name="den_ps")
-        z_ps = single_banks.tile([C, M], F32, name="z_ps")
+        z_ps = z_bank.tile([C, M], F32, name="z_ps")
 
         def add_blocks(pair, blocks):
             for a in blocks:
@@ -169,9 +166,10 @@ def tile_gatedge_kernel(tc, x, edge, w_edge, attn_l, attn_r, dst, offs, out):
             both = slice(first, first + PAIR)
             nc.vector.tensor_tensor(weights[:, both, 0:BLOCKS], p_pos[:, both, :], p_neg[:, both, :], ALU.max)
             nc.vector.tensor_reduce(row_sum[:, both], weights[:, both, :], AXIS.X, ALU.add)
-            nc.tensor.matmul(den_ps[:, both], same_machine[:], row_sum[:, both], start=True, stop=True)
+            den_ps = column_banks.tile([ROWS, PAIR], F32, name="den_ps", tag="columns")
+            nc.tensor.matmul(den_ps[:], same_machine[:], row_sum[:, both], start=True, stop=True)
             add_blocks(pair, range(0, BLOCKS // 2))
-            nc.vector.reciprocal(rden[:, both], den_ps[:, both])
+            nc.vector.reciprocal(rden[:, both], den_ps[:])
             for r in pair:
                 nc.scalar.activation(fold[:, r, :], row_of_machine, FUNC.Copy, scale=rden[:, r : r + 1])
             add_blocks(pair, range(BLOCKS // 2, BLOCKS))

@@ -39,6 +39,8 @@ def tile_gatedge_kernel(tc, x, edge, w_edge, attn_l, attn_r, dst, offs, out):
     ):
         w_edge_col = held.tile([C, 1], F32, name="w_edge_col")
         nc.scalar.dma_start(w_edge_col[:], w_edge)
+        dst_f32 = held.tile([C, M], F32, name="dst_f32")
+        nc.sync.dma_start(dst_f32[:], dst)
         table = held.tile([C, S], F32, name="table")
         nc.sync.dma_start(table[:], x)
         offsets = held.tile([C, N // PER_COLUMN], U16, name="offsets")
@@ -49,8 +51,6 @@ def tile_gatedge_kernel(tc, x, edge, w_edge, attn_l, attn_r, dst, offs, out):
         attn_l_col = held.tile([C, 1], F32, name="attn_l_col")
         nc.scalar.dma_start(attn_l_col[:], attn_l)
         nc.scalar.dma_start(edge_all[:, half:N], edge[0, half:N].partition_broadcast(C))
-        dst_f32 = held.tile([C, M], F32, name="dst_f32")
-        nc.sync.dma_start(dst_f32[:], dst)
         attn_r_col = held.tile([C, 1], F32, name="attn_r_col")
         nc.sync.dma_start(attn_r_col[:], attn_r)
         scratch = held.tile([C, 1], F32, name="scratch")
@@ -85,14 +85,6 @@ def tile_gatedge_kernel(tc, x, edge, w_edge, attn_l, attn_r, dst, offs, out):
         nc.gpsimd.tensor_copy(attn_r_bf, attn_r_col[:])
         nc.gpsimd.tensor_copy(attn_l_bf, attn_l_col[:])
 
-        we_of = []
-        for r in range(N_PIECES):
-            we = pieces.tile([C, PIECE], F32, name="we")
-            nc.scalar.activation(
-                we[:], edge_all[:, r * PIECE : (r + 1) * PIECE], FUNC.Copy, scale=w_edge_col[:, 0:1]
-            )
-            we_of.append(we)
-
         dst_wide = dst_f32[:].unsqueeze(2).to_broadcast([C, M, SHARE])
         dst_rep_bf = held.tile([C, M, SHARE], BF16, name="dst_rep_bf")
         nc.vector.tensor_copy(dst_rep_bf[:], dst_wide)
@@ -100,6 +92,17 @@ def tile_gatedge_kernel(tc, x, edge, w_edge, attn_l, attn_r, dst, offs, out):
         nc.vector.tensor_copy(dst_rep[:], dst_wide)
         dst_rep_bf_blocks = dst_rep_bf[:].rearrange("c m u -> c (m u)")
         dst_rep_blocks = dst_rep[:].rearrange("c m u -> c (m u)")
+
+        we_of = []
+        for r in range(N_PIECES):
+            we = pieces.tile([C, PIECE], F32, name="we")
+            edge_piece = edge_all[:, r * PIECE : (r + 1) * PIECE]
+            if r == 0:
+                nc.vector.tensor_scalar(we[:], edge_piece, w_edge_col[:, 0:1], None, ALU.mult)
+            else:
+                nc.scalar.activation(we[:], edge_piece, FUNC.Copy, scale=w_edge_col[:, 0:1])
+            we_of.append(we)
+
         er_ps = column_banks.tile([ROWS, N_PIECES], F32, name="er_ps", tag="columns")
         dst_flipped = flip_banks.tile([ROWS, N_PIECES, C], F32, name="dst_flipped", tag="flipped")
         for r in range(N_PIECES):

import math

import concourse.mybir as mybir

F32 = mybir.dt.float32
BF16 = mybir.dt.bfloat16
U16 = mybir.dt.uint16
ALU = mybir.AluOpType
FUNC = mybir.ActivationFunctionType
AXIS = mybir.AxisListType

C = 128
S = 1024
N = 2048
M = 128
E = 16
PER_COLUMN = 16
PIECE = 512
N_PIECES = N // PIECE
MACH = PIECE // E
ROWS = 128
BLOCKS = PIECE // ROWS
SHARE = ROWS // MACH
PAIR = 2
SLOPE = 0.2
LOG_SHARE_OF_ROW = -math.log(SHARE)

FLOPS = 2 * C * N + 2 * C * M + 2 * C * N


def tile_gatedge_kernel(tc, x, edge, w_edge, attn_l, attn_r, dst, offs, out):
    nc = tc.nc
    with (
        tc.tile_pool(name="held", bufs=1) as held,
        tc.tile_pool(name="pieces", bufs=N_PIECES) as pieces,
        tc.psum_pool(name="flip_banks", bufs=N_PIECES + 1) as flip_banks,
        tc.psum_pool(name="column_banks", bufs=2) as column_banks,
        tc.psum_pool(name="z_bank", bufs=1) as z_bank,
    ):
        w_edge_col = held.tile([C, 1], F32, name="w_edge_col")
        nc.scalar.dma_start(w_edge_col[:], w_edge)
        dst_f32 = held.tile([C, M], F32, name="dst_f32")
        nc.sync.dma_start(dst_f32[:], dst)
        table = held.tile([C, S], F32, name="table")
        nc.sync.dma_start(table[:], x)
        offsets = held.tile([C, N // PER_COLUMN], U16, name="offsets")
        nc.sync.dma_start(offsets[:], offs)
        edge_all = held.tile([C, N], F32, name="edge_all")
        half = N // 2
        nc.scalar.dma_start(edge_all[:, 0:half], edge[0, 0:half].partition_broadcast(C))
        attn_l_col = held.tile([C, 1], F32, name="attn_l_col")
        nc.scalar.dma_start(attn_l_col[:], attn_l)
        nc.scalar.dma_start(edge_all[:, half:N], edge[0, half:N].partition_broadcast(C))
        attn_r_col = held.tile([C, 1], F32, name="attn_r_col")
        nc.sync.dma_start(attn_r_col[:], attn_r)
        scratch = held.tile([C, 1], F32, name="scratch")
        nc.vector.memset(scratch[:], 0.0)
        nc.scalar.activation(scratch[:], scratch[:], FUNC.Exp)

        one = held.tile([1, 1], F32, name="one")
        nc.vector.memset(one[:], 1.0)
        all_ones = held.tile([C, C], F32, name="all_ones")
        nc.vector.memset(all_ones[:], 1.0)
        first_of_machine = held.tile([ROWS, MACH, SHARE], F32, name="first_of_machine")
        nc.vector.memset(first_of_machine[:], 0.0)
        nc.vector.memset(first_of_machine[:, :, 0], 1.0)
        column_number = held.tile([C, C], F32, name="column_number")
        nc.vector.tensor_tensor_scan(column_number[:], all_ones[:], all_ones[:], 0.0, ALU.mult, ALU.add)
        column_machine = held.tile([ROWS, ROWS], F32, name="column_machine")
        nc.vector.tensor_tensor_scan(
            column_machine[:], all_ones[:], first_of_machine[:].rearrange("i m u -> i (m u)"), 0.0, ALU.mult, ALU.add
        )
        partition_ps = column_banks.tile([C, 2], F32, name="partition_ps", tag="columns")
        nc.tensor.matmul(partition_ps[:, 0:1], column_number[0:1, :], one[:], start=True, stop=True)
        nc.tensor.matmul(partition_ps[:, 1:2], column_machine[0:1, :], one[:], start=True, stop=True)
        identity = held.tile([C, C], F32, name="identity")
        nc.vector.tensor_scalar(identity[:], column_number[:], partition_ps[:, 0:1], None, ALU.is_equal)
        same_machine = held.tile([ROWS, ROWS], F32, name="same_machine")
        nc.vector.tensor_scalar(same_machine[:], column_machine[:], partition_ps[:, 1:2], None, ALU.is_equal)
        row_of_machine = same_machine[:].rearrange("i (m u) -> i u m", u=SHARE)[:, 0, :]

        attn_bf = held.tile([C, 2], BF16, name="attn_bf")
        attn_r_bf = attn_bf[:, 0:1]
        attn_l_bf = attn_bf[:, 1:2]
        nc.gpsimd.tensor_copy(attn_r_bf, attn_r_col[:])
        nc.gpsimd.tensor_copy(attn_l_bf, attn_l_col[:])

        dst_wide = dst_f32[:].unsqueeze(2).to_broadcast([C, M, SHARE])
        dst_rep_bf = held.tile([C, M, SHARE], BF16, name="dst_rep_bf")
        nc.vector.tensor_copy(dst_rep_bf[:], dst_wide)
        dst_rep = held.tile([C, M, SHARE], F32, name="dst_rep")
        nc.vector.tensor_copy(dst_rep[:], dst_wide)
        dst_rep_bf_blocks = dst_rep_bf[:].rearrange("c m u -> c (m u)")
        dst_rep_blocks = dst_rep[:].rearrange("c m u -> c (m u)")

        we_of = []
        for r in range(N_PIECES):
            we = pieces.tile([C, PIECE], F32, name="we")
            edge_piece = edge_all[:, r * PIECE : (r + 1) * PIECE]
            if r == 0:
                nc.vector.tensor_scalar(we[:], edge_piece, w_edge_col[:, 0:1], None, ALU.mult)
            else:
                nc.scalar.activation(we[:], edge_piece, FUNC.Copy, scale=w_edge_col[:, 0:1])
            we_of.append(we)

        er_ps = column_banks.tile([ROWS, N_PIECES], F32, name="er_ps", tag="columns")
        dst_flipped = flip_banks.tile([ROWS, N_PIECES, C], F32, name="dst_flipped", tag="flipped")
        for r in range(N_PIECES):
            rows = slice(r * ROWS, (r + 1) * ROWS)
            nc.tensor.matmul(er_ps[:, r : r + 1], dst_rep_bf_blocks[:, rows], attn_r_bf, start=True, stop=True)
        for r in range(N_PIECES):
            rows = slice(r * ROWS, (r + 1) * ROWS)
            nc.tensor.transpose(dst_flipped[:, r, :], dst_rep_blocks[:, rows], identity[:])
        er = held.tile([ROWS, N_PIECES], F32, name="er")
        nc.scalar.copy(er[:], er_ps[:])
        er_slope = held.tile([ROWS, N_PIECES], F32, name="er_slope")
        nc.scalar.mul(er_slope[:], er_ps[:], SLOPE)
        weights = held.tile([ROWS, N_PIECES, BLOCKS + 1], F32, name="weights")
        er_relu = held.tile([ROWS, N_PIECES], F32, name="er_relu")
        nc.scalar.activation(er_relu[:], er_ps[:], FUNC.Relu, scale=2.0 * (1.0 - SLOPE))
        er_shifted = held.tile([ROWS, N_PIECES], F32, name="er_shifted")
        nc.scalar.add(er_shifted[:], er_ps[:], LOG_SHARE_OF_ROW / (2.0 * SLOPE))
        acc_of = []
        for r in range(N_PIECES):
            own_weight = weights[:, r, BLOCKS : BLOCKS + 1]
            nc.scalar.activation(own_weight, er_shifted[:, r : r + 1], FUNC.Exp, bias=er_relu[:, r : r + 1], scale=2.0 * SLOPE)
            acc = pieces.tile([ROWS, C], F32, name="acc")
            nc.scalar.activation(acc[:], dst_flipped[:, r, :], FUNC.Copy, scale=own_weight)
            acc_of.append(acc)

        p_pos = held.tile([ROWS, N_PIECES, BLOCKS], F32, name="p_pos")
        p_neg = held.tile([ROWS, N_PIECES, BLOCKS], F32, name="p_neg")
        flipped_of = []
        for r in range(N_PIECES):
            wmu = pieces.tile([C, PIECE], F32, name="wmu")
            picked = table[:].indirect(offsets[:, r * (PIECE // PER_COLUMN) : (r + 1) * (PIECE // PER_COLUMN)])
            nc.vector.tensor_tensor(wmu[:], picked, we_of[r][:], ALU.add)
            wmu_blocks = wmu[:].rearrange("c (i a) -> c a i", a=BLOCKS)
            wmu_bf = pieces.tile([C, PIECE], BF16, name="wmu_bf")
            if r == N_PIECES - 1:
                nc.vector.tensor_copy(wmu_bf[:], wmu[:])
            else:
                nc.scalar.copy(wmu_bf[:], wmu[:])
            wmu_bf_blocks = wmu_bf[:].rearrange("c (i a) -> c a i", a=BLOCKS)
            flipped = flip_banks.tile([ROWS, BLOCKS, C], F32, name="flipped", tag="flipped")
            for a in range(BLOCKS):
                nc.tensor.transpose(flipped[:, a, :], wmu_blocks[:, a, :], identity[:])
            flipped_of.append(flipped)
            s_ps = column_banks.tile([ROWS, BLOCKS], F32, name="s_ps", tag="columns")
            for a in range(BLOCKS):
                nc.tensor.matmul(s_ps[:, a : a + 1], wmu_bf_blocks[:, a, :], attn_l_bf, start=True, stop=True)
            nc.scalar.activation(p_pos[:, r, :], s_ps[:], FUNC.Exp, bias=er[:, r : r + 1], scale=1.0)
            nc.scalar.activation(p_neg[:, r, :], s_ps[:], FUNC.Exp, bias=er_slope[:, r : r + 1], scale=SLOPE)

        row_sum = held.tile([ROWS, N_PIECES], F32, name="row_sum")
        rden = held.tile([ROWS, N_PIECES], F32, name="rden")
        fold = held.tile([ROWS, N_PIECES, MACH], F32, name="fold")
        z_ps = z_bank.tile([C, M], F32, name="z_ps")

        def add_blocks(pair, blocks):
            for a in blocks:
                for r in pair:
                    nc.vector.scalar_tensor_tensor(
                        acc_of[r][:], flipped_of[r][:, a, :], weights[:, r, a : a + 1], acc_of[r][:], ALU.mult, ALU.add
                    )

        for first in range(0, N_PIECES, PAIR):
            pair = range(first, first + PAIR)
            both = slice(first, first + PAIR)
            nc.vector.tensor_tensor(weights[:, both, 0:BLOCKS], p_pos[:, both, :], p_neg[:, both, :], ALU.max)
            nc.vector.tensor_reduce(row_sum[:, both], weights[:, both, :], AXIS.X, ALU.add)
            den_ps = column_banks.tile([ROWS, PAIR], F32, name="den_ps", tag="columns")
            nc.tensor.matmul(den_ps[:], same_machine[:], row_sum[:, both], start=True, stop=True)
            add_blocks(pair, range(0, BLOCKS // 2))
            nc.vector.reciprocal(rden[:, both], den_ps[:])
            for r in pair:
                nc.scalar.activation(fold[:, r, :], row_of_machine, FUNC.Copy, scale=rden[:, r : r + 1])
            add_blocks(pair, range(BLOCKS // 2, BLOCKS))
            for r in pair:
                nc.tensor.matmul(z_ps[:, r * MACH : (r + 1) * MACH], acc_of[r][:], fold[:, r, :], start=True, stop=True)

        result = held.tile([C, M], F32, name="result")
        nc.scalar.activation(result[:], z_ps[:], FUNC.Sigmoid)
        nc.sync.dma_start(out, result[:])
